import numpy as np
import ml_dtypes


def mxq(x, axis, fmt="e4m3"):
    dtype, down = {"e4m3": (ml_dtypes.float8_e4m3fn, 7), "e5m2": (ml_dtypes.float8_e5m2, 14)}[fmt]
    v = np.moveaxis(np.asarray(x, np.float32).astype(ml_dtypes.bfloat16).astype(np.float64), axis, -1)
    blocks = v.reshape(v.shape[:-1] + (-1, 32))
    amax = np.abs(blocks).max(-1, keepdims=True)
    byte = np.maximum(np.where(amax > 0, np.frexp(amax)[1] - 1 + 127, 0) - down, 1)
    scale = np.exp2(byte - 127.0)
    codes = (blocks / scale).astype(np.float32).astype(dtype).astype(np.float64)
    return np.moveaxis((codes * scale).reshape(v.shape), -1, axis)


WIDE = False


def mx_kscale(k):
    if not WIDE:
        return np.ones(k)
    levels = np.array([10, -10, 5, -5, 0])
    a = np.random.permutation(np.resize(levels, k // 512 * 4)).reshape(k // 512, 4)
    idx = np.arange(k)
    return np.exp2(a[idx // 512, idx % 128 // 32])


BF16 = ml_dtypes.bfloat16


def bf(x):
    return np.asarray(x, np.float32).astype(BF16)


def f64(x):
    return np.asarray(x).astype(np.float64)


N, DIM, DIM_INNER, T, H, W = 4, 256, 512, 8, 16, 16
L = T * H * W
EPS = 1e-5


def setup_inputs():
    s = mx_kscale(DIM_INNER)
    return {"x": bf(np.random.standard_normal((N, DIM, T, H, W))),
            "attn_out": bf(np.random.standard_normal((N, DIM_INNER, T, H, W)) * 0.25 * s[None, :, None, None, None]),
            "w_out": bf(np.random.standard_normal((DIM, DIM_INNER)) * 3.0 / np.sqrt(DIM_INNER) / s[None, :]),
            "b_out": bf(0.3 + np.random.standard_normal(DIM) * 0.4)}


def reference(x, attn_out, w_out, b_out):
    a = f64(attn_out).reshape(N, DIM_INNER, L)
    p = (mxq(f64(w_out), 1, "e4m3") @ mxq(a, 1, "e4m3")) + f64(b_out)[None, :, None]
    mu = p.mean(axis=(1, -1), keepdims=True)
    var = p.var(axis=(1, -1), keepdims=True)
    p = (p - mu) / np.sqrt(var + EPS)
    return f64(x) + p.reshape(N, DIM, T, H, W)

@@ -1,0 +1,268 @@
+from contextlib import ExitStack
+
+import concourse.mybir as mybir
+from concourse.masks import make_identity
+
+F32 = mybir.dt.float32
+BF16 = mybir.dt.bfloat16
+U32 = mybir.dt.uint32
+U8 = mybir.dt.uint8
+FP8X4 = mybir.dt.float8_e4m3fn_x4
+ACT = mybir.ActivationFunctionType
+ALU = mybir.AluOpType
+
+SAMPLES = 4
+C_IN = 512
+C_OUT = 256
+POSITIONS = 2048
+EPS = 1e-5
+
+P = 128
+PACK = 4
+COLS = 512
+CHUNKS = POSITIONS // COLS
+HALVES = C_OUT // P
+STATS = 6
+VECTOR_COLS = 64
+
+QUANTISE_LAG = 1
+SUM_LAG = 2
+NORMALISE_LAG = 9
+
+FLOPS = 2 * SAMPLES * C_OUT * C_IN * POSITIONS
+
+
+def tile_prgselfatt_pa_t_kernel(tc, x, attn_out, w_out, b_out, out):
+    nc = tc.nc
+    with ExitStack() as ctx:
+        const = ctx.enter_context(tc.tile_pool(name="const", bufs=1))
+        inputs = ctx.enter_context(tc.tile_pool(name="inputs", bufs=1))
+        stage = ctx.enter_context(tc.tile_pool(name="stage", bufs=3))
+        small = ctx.enter_context(tc.tile_pool(name="small", bufs=2))
+        results = ctx.enter_context(tc.tile_pool(name="results", bufs=6))
+        psum_small = ctx.enter_context(tc.psum_pool(name="psum_small", bufs=1))
+        psum_sum = ctx.enter_context(tc.psum_pool(name="psum_sum", bufs=3))
+        psum_norm = ctx.enter_context(tc.psum_pool(name="psum_norm", bufs=4))
+        a_raw = []
+        x_rows = []
+        a_codes = []
+        a_scales = []
+        for n in range(SAMPLES):
+            a_raw.append(inputs.tile([P, PACK, POSITIONS], BF16, name="a_raw%d" % n))
+            x_rows.append(inputs.tile([P, HALVES, POSITIONS], BF16, name="x_rows%d" % n))
+            a_codes.append(inputs.tile([P, POSITIONS], U32, name="a_codes%d" % n, align_bytes=64))
+            a_scales.append(inputs.tile([P, POSITIONS], U8, name="a_scales%d" % n, align_bytes=64))
+        w_rows = const.tile([P, HALVES, C_IN], BF16)
+        b_rows = const.tile([P, P], BF16)
+        nc.vector.memset(b_rows[:], 0.0)
+
+        def load_a(n, q):
+            cols = slice(q * COLS, (q + 1) * COLS)
+            rows = attn_out[n].rearrange("(p j) t y w -> p j (t y w)", j=PACK)
+            nc.sync.dma_start(out=a_raw[n][:, :, cols], in_=rows[:, :, cols])
+
+        for n in range(SAMPLES):
+            for q in range(CHUNKS):
+                load_a(n, q)
+                if (n, q) == (0, 0):
+                    nc.sync.dma_start(
+                        out=w_rows[:], in_=w_out.rearrange("(h c) k -> c h k", h=HALVES)
+                    )
+                    nc.sync.dma_start(
+                        out=b_rows[0:HALVES, :], in_=b_out.rearrange("(h c) -> h c", h=HALVES)
+                    )
+            if n > 0:
+                nc.sync.dma_start(
+                    out=x_rows[n - 1][:],
+                    in_=x[n - 1].rearrange("(h c) t y w -> c h (t y w)", h=HALVES),
+                )
+        nc.sync.dma_start(
+            out=x_rows[SAMPLES - 1][:],
+            in_=x[SAMPLES - 1].rearrange("(h c) t y w -> c h (t y w)", h=HALVES),
+        )
+
+        ident = const.tile([P, P], F32)
+        make_identity(nc, ident[:])
+        mean_over_partitions = const.tile([P, P], F32)
+        nc.vector.memset(mean_over_partitions[:], 1.0 / P)
+        one = const.tile([P, 1], F32)
+        nc.vector.memset(one[:], 1.0)
+        nc.scalar.activation(out=one[:], in_=one[:], func=ACT.Sqrt)
+
+        w_words = (
+            w_rows[:]
+            .rearrange("c h k -> c (h k)")
+            .bitcast(F32)
+            .rearrange("c (h p u) -> c h u p", h=HALVES, u=2)
+        )
+        w_t = psum_small.tile([P, 2, C_OUT], F32, tag="small")
+        for h in range(HALVES):
+            for u in range(2):
+                nc.tensor.transpose(w_t[:, u, h * P : (h + 1) * P], w_words[:, h, u, :], ident[:])
+        w_grouped = const.tile([P, C_OUT * PACK], BF16, align_bytes=64)
+        nc.vector.tensor_copy(
+            out=w_grouped[:].bitcast(F32).rearrange("p (c u) -> p c u", u=2),
+            in_=w_t[:].rearrange("p u c -> p c u"),
+        )
+        w_codes = const.tile([P, C_OUT], U32, align_bytes=64)
+        w_scales = const.tile([P, C_OUT], U8, align_bytes=64)
+        nc.vector.quantize_mx(out=w_codes[:].bitcast(FP8X4), scales=w_scales[:], in_=w_grouped[:])
+
+        b_rows32 = const.tile([P, P], F32)
+        nc.vector.tensor_copy(out=b_rows32[:], in_=b_rows[:])
+        b_t = psum_small.tile([P, P], F32, tag="small")
+        nc.tensor.transpose(b_t[:], b_rows32[:], ident[:])
+        b_col = const.tile([P, HALVES], F32)
+        nc.vector.tensor_copy(out=b_col[:], in_=b_t[:, 0:HALVES])
+
+        grouped = {}
+        stats = {}
+        totals = {}
+        scale_shift = {}
+
+        def regroup(n, q):
+            tile = stage.tile([P, COLS, PACK], BF16, name="grouped", align_bytes=64)
+            rows = a_raw[n][:, :, q * COLS : (q + 1) * COLS]
+            for copy, first, last in (
+                (nc.vector.tensor_copy, 0, VECTOR_COLS),
+                (nc.scalar.copy, VECTOR_COLS, COLS),
+            ):
+                copy(
+                    out=tile[:, first:last, :].rearrange("p (c i) j -> p c j i", i=4),
+                    in_=rows[:, :, first:last].rearrange("p j (c i) -> p c j i", i=4),
+                )
+            grouped[(n, q)] = tile
+
+        def quantise(n, q):
+            cols = slice(q * COLS, (q + 1) * COLS)
+            nc.vector.quantize_mx(
+                out=a_codes[n][:, cols].bitcast(FP8X4),
+                scales=a_scales[n][:, cols],
+                in_=grouped[(n, q)][:].rearrange("p w j -> p (w j)"),
+            )
+
+        def multiply(pool, n, q, h):
+            cols = slice(q * COLS, (q + 1) * COLS)
+            channels = slice(h * P, (h + 1) * P)
+            product = pool.tile([P, COLS], F32, name="product")
+            nc.tensor.matmul_mx(
+                out=product[:],
+                lhsT=w_codes[:, channels].bitcast(FP8X4),
+                lhsT_scale=w_scales[:, channels],
+                rhs=a_codes[n][:, cols].bitcast(FP8X4),
+                rhs_scale=a_scales[n][:, cols],
+                start=True,
+                stop=True,
+            )
+            return product
+
+        def sum_chunk(n, q):
+            if q == 0:
+                stats[n] = small.tile([P, HALVES, CHUNKS, STATS], F32, name="stats")
+            for h in range(HALVES):
+                product = multiply(psum_sum, n, q, h)
+                nc.vector.bn_stats(out=stats[n][:, h, q, :], in_=product[:])
+
+        def sum_sample(n):
+            means = stats[n][:].rearrange("p h q (e s) -> p h (q e) s", s=3)[:, :, :, 1]
+            nc.vector.tensor_tensor(
+                out=means,
+                in0=means,
+                in1=b_col[:].unsqueeze(2).to_broadcast([P, HALVES, 2 * CHUNKS]),
+                op=ALU.add,
+            )
+            moments = small.tile([P, 2], F32)
+            nc.vector.bn_aggr(out=moments[:], in_=stats[n][:].rearrange("p h q s -> p (h q s)"))
+            nc.vector.scalar_tensor_tensor(
+                out=moments[:, 1:2],
+                in0=moments[:, 0:1],
+                scalar=moments[:, 0:1],
+                in1=moments[:, 1:2],
+                op0=ALU.mult,
+                op1=ALU.add,
+            )
+            total_ps = psum_small.tile([P, 2], F32, tag="small")
+            nc.tensor.matmul(
+                out=total_ps[:], lhsT=mean_over_partitions[:], rhs=moments[:], start=True, stop=True
+            )
+            return total_ps
+
+        def variance(n, total_ps):
+            total = small.tile([P, 2], F32)
+            nc.vector.tensor_copy(out=total[:], in_=total_ps[:])
+            neg_var = small.tile([P, 1], F32)
+            nc.vector.scalar_tensor_tensor(
+                out=neg_var[:],
+                in0=total[:, 0:1],
+                scalar=total[:, 0:1],
+                in1=total[:, 1:2],
+                op0=ALU.mult,
+                op1=ALU.subtract,
+            )
+            totals[n] = (total, neg_var)
+
+        def scale_and_shift(n):
+            total, neg_var = totals[n]
+            std = small.tile([P, 1], F32)
+            nc.scalar.activation(out=std[:], in_=neg_var[:], func=ACT.Sqrt, scale=-1.0, bias=EPS)
+            rstd = small.tile([P, 1], F32)
+            nc.vector.reciprocal(out=rstd[:], in_=std[:])
+            shift = small.tile([P, HALVES], F32)
+            nc.vector.tensor_scalar(
+                out=shift[:],
+                in0=b_col[:],
+                scalar1=total[:, 0:1],
+                scalar2=rstd[:, 0:1],
+                op0=ALU.subtract,
+                op1=ALU.mult,
+            )
+            scale_shift[n] = (rstd, shift)
+
+        def normalise(n, q):
+            rstd, shift = scale_shift[n]
+            result = results.tile([P, HALVES, COLS], F32)
+            for h in range(HALVES):
+                product = multiply(psum_norm, n, q, h)
+                nc.scalar.activation(
+                    out=result[:, h, :],
+                    in_=product[:],
+                    func=ACT.Identity,
+                    scale=rstd[:, 0:1],
+                    bias=shift[:, h : h + 1],
+                )
+            return result
+
+        def add_x_and_store(n, q, result):
+            cols = slice(q * COLS, (q + 1) * COLS)
+            nc.vector.tensor_tensor(
+                out=result[:], in0=result[:], in1=x_rows[n][:, :, cols], op=ALU.add
+            )
+            nc.sync.dma_start(
+                out=out[n].rearrange("(h c) t y w -> c h (t y w)", h=HALVES)[:, :, cols],
+                in_=result[:],
+            )
+
+        total_chunks = SAMPLES * CHUNKS
+        for step in range(total_chunks + NORMALISE_LAG):
+            to_regroup = step
+            to_quantise = step - QUANTISE_LAG
+            to_sum = step - SUM_LAG
+            to_normalise = step - NORMALISE_LAG
+
+            if 0 <= to_quantise < total_chunks:
+                quantise(*divmod(to_quantise, CHUNKS))
+            if 0 <= to_sum - 2 < total_chunks and (to_sum - 2) % CHUNKS == CHUNKS - 1:
+                scale_and_shift((to_sum - 2) // CHUNKS)
+            if to_normalise >= 0:
+                result = normalise(*divmod(to_normalise, CHUNKS))
+            if to_regroup < total_chunks:
+                regroup(*divmod(to_regroup, CHUNKS))
+            sample_done = 0 <= to_sum < total_chunks and to_sum % CHUNKS == CHUNKS - 1
+            if 0 <= to_sum < total_chunks:
+                sum_chunk(*divmod(to_sum, CHUNKS))
+            if sample_done:
+                total_ps = sum_sample(to_sum // CHUNKS)
+            if to_normalise >= 0:
+                add_x_and_store(*divmod(to_normalise, CHUNKS), result)
+            if sample_done:
+                variance(to_sum // CHUNKS, total_ps)

@@ -10,6 +10,7 @@ U8 = mybir.dt.uint8
 FP8X4 = mybir.dt.float8_e4m3fn_x4
 ACT = mybir.ActivationFunctionType
 ALU = mybir.AluOpType
+X_AXIS = mybir.AxisListType.X
 
 SAMPLES = 4
 C_IN = 512
@@ -22,8 +23,7 @@ PACK = 4
 COLS = 512
 CHUNKS = POSITIONS // COLS
 HALVES = C_OUT // P
-STATS = 6
-VECTOR_COLS = 64
+SCALAR_COLS = 80
 
 QUANTISE_LAG = 1
 SUM_LAG = 2
@@ -41,8 +41,9 @@ def tile_prgselfatt_pa_t_kernel(tc, x, attn_out, w_out, b_out, out):
         small = ctx.enter_context(tc.tile_pool(name="small", bufs=2))
         results = ctx.enter_context(tc.tile_pool(name="results", bufs=6))
         psum_small = ctx.enter_context(tc.psum_pool(name="psum_small", bufs=1))
-        psum_sum = ctx.enter_context(tc.psum_pool(name="psum_sum", bufs=3))
-        psum_norm = ctx.enter_context(tc.psum_pool(name="psum_norm", bufs=4))
+        psum_mean = ctx.enter_context(tc.psum_pool(name="psum_mean", bufs=2))
+        psum_square = ctx.enter_context(tc.psum_pool(name="psum_square", bufs=2))
+        psum_norm = ctx.enter_context(tc.psum_pool(name="psum_norm", bufs=3))
         a_raw = []
         x_rows = []
         a_codes = []
@@ -61,30 +62,24 @@ def tile_prgselfatt_pa_t_kernel(tc, x, attn_out, w_out, b_out, out):
             rows = attn_out[n].rearrange("(p j) t y w -> p j (t y w)", j=PACK)
             nc.sync.dma_start(out=a_raw[n][:, :, cols], in_=rows[:, :, cols])
 
-        for n in range(SAMPLES):
-            for q in range(CHUNKS):
-                load_a(n, q)
-                if (n, q) == (0, 0):
-                    nc.sync.dma_start(
-                        out=w_rows[:], in_=w_out.rearrange("(h c) k -> c h k", h=HALVES)
-                    )
-                    nc.sync.dma_start(
-                        out=b_rows[0:HALVES, :], in_=b_out.rearrange("(h c) -> h c", h=HALVES)
-                    )
-            if n > 0:
-                nc.sync.dma_start(
-                    out=x_rows[n - 1][:],
-                    in_=x[n - 1].rearrange("(h c) t y w -> c h (t y w)", h=HALVES),
-                )
-        nc.sync.dma_start(
-            out=x_rows[SAMPLES - 1][:],
-            in_=x[SAMPLES - 1].rearrange("(h c) t y w -> c h (t y w)", h=HALVES),
-        )
+        def load_x(n):
+            nc.sync.dma_start(
+                out=x_rows[n][:], in_=x[n].rearrange("(h c) t y w -> c h (t y w)", h=HALVES)
+            )
+
+        load_a(0, 0)
+        nc.sync.dma_start(out=w_rows[:], in_=w_out.rearrange("(h c) k -> c h k", h=HALVES))
+        nc.sync.dma_start(out=b_rows[0:HALVES, :], in_=b_out.rearrange("(h c) -> h c", h=HALVES))
+        for chunk in range(1, SAMPLES * CHUNKS + NORMALISE_LAG):
+            if chunk >= NORMALISE_LAG and (chunk - NORMALISE_LAG) % CHUNKS == 0:
+                load_x((chunk - NORMALISE_LAG) // CHUNKS)
+            if chunk < SAMPLES * CHUNKS:
+                load_a(*divmod(chunk, CHUNKS))
 
         ident = const.tile([P, P], F32)
         make_identity(nc, ident[:])
-        mean_over_partitions = const.tile([P, P], F32)
-        nc.vector.memset(mean_over_partitions[:], 1.0 / P)
+        mean_of_sample = const.tile([P, P], F32)
+        nc.vector.memset(mean_of_sample[:], 1.0 / (C_OUT * POSITIONS))
         one = const.tile([P, 1], F32)
         nc.vector.memset(one[:], 1.0)
         nc.scalar.activation(out=one[:], in_=one[:], func=ACT.Sqrt)
@@ -114,24 +109,39 @@ def tile_prgselfatt_pa_t_kernel(tc, x, attn_out, w_out, b_out, out):
         nc.tensor.transpose(b_t[:], b_rows32[:], ident[:])
         b_col = const.tile([P, HALVES], F32)
         nc.vector.tensor_copy(out=b_col[:], in_=b_t[:, 0:HALVES])
+        b_mean_ps = psum_small.tile([P, HALVES], F32, tag="small")
+        nc.tensor.matmul(
+            out=b_mean_ps[:], lhsT=mean_of_sample[:], rhs=b_col[:], start=True, stop=True
+        )
+        b_mean = const.tile([P, 1], F32)
+        nc.vector.tensor_reduce(out=b_mean[:], in_=b_mean_ps[:], axis=X_AXIS, op=ALU.add)
+        b_centred = const.tile([P, HALVES], F32)
+        nc.vector.scalar_tensor_tensor(
+            out=b_centred[:],
+            in0=b_mean[:].to_broadcast([P, HALVES]),
+            scalar=-float(POSITIONS),
+            in1=b_col[:],
+            op0=ALU.mult,
+            op1=ALU.add,
+        )
 
         grouped = {}
-        stats = {}
+        square_sums = {}
+        position_sums = {}
         totals = {}
         scale_shift = {}
 
         def regroup(n, q):
-            tile = stage.tile([P, COLS, PACK], BF16, name="grouped", align_bytes=64)
+            grouped[(n, q)] = stage.tile([P, COLS, PACK], BF16, name="grouped", align_bytes=64)
             rows = a_raw[n][:, :, q * COLS : (q + 1) * COLS]
             for copy, first, last in (
-                (nc.vector.tensor_copy, 0, VECTOR_COLS),
-                (nc.scalar.copy, VECTOR_COLS, COLS),
+                (nc.scalar.copy, 0, SCALAR_COLS),
+                (nc.vector.tensor_copy, SCALAR_COLS, COLS),
             ):
                 copy(
-                    out=tile[:, first:last, :].rearrange("p (c i) j -> p c j i", i=4),
+                    out=grouped[(n, q)][:, first:last, :].rearrange("p (c i) j -> p c j i", i=4),
                     in_=rows[:, :, first:last].rearrange("p j (c i) -> p c j i", i=4),
                 )
-            grouped[(n, q)] = tile
 
         def quantise(n, q):
             cols = slice(q * COLS, (q + 1) * COLS)
@@ -158,32 +168,39 @@ def tile_prgselfatt_pa_t_kernel(tc, x, attn_out, w_out, b_out, out):
 
         def sum_chunk(n, q):
             if q == 0:
-                stats[n] = small.tile([P, HALVES, CHUNKS, STATS], F32, name="stats")
+                square_sums[n] = small.tile([P, CHUNKS * HALVES], F32, name="square_sums")
+                position_sums[n] = psum_mean.tile([P, C_OUT], F32, name="position_sums")
             for h in range(HALVES):
-                product = multiply(psum_sum, n, q, h)
-                nc.vector.bn_stats(out=stats[n][:, h, q, :], in_=product[:])
+                product = multiply(psum_square, n, q, h)
+                squares = stage.tile([P, COLS], BF16)
+                bank = q * HALVES + h
+                nc.scalar.activation(
+                    out=squares[:],
+                    in_=product[:],
+                    func=ACT.Square,
+                    bias=b_centred[:, h : h + 1],
+                    accum_out=square_sums[n][:, bank : bank + 1],
+                )
+            for first in range(q * COLS, (q + 1) * COLS, P):
+                nc.tensor.matmul_mx(
+                    out=position_sums[n][:],
+                    lhsT=a_codes[n][:, first : first + P].bitcast(FP8X4),
+                    lhsT_scale=a_scales[n][:, first : first + P],
+                    rhs=w_codes[:].bitcast(FP8X4),
+                    rhs_scale=w_scales[:],
+                    start=(first == 0),
+                    stop=(first + P == POSITIONS),
+                )
 
         def sum_sample(n):
-            means = stats[n][:].rearrange("p h q (e s) -> p h (q e) s", s=3)[:, :, :, 1]
-            nc.vector.tensor_tensor(
-                out=means,
-                in0=means,
-                in1=b_col[:].unsqueeze(2).to_broadcast([P, HALVES, 2 * CHUNKS]),
-                op=ALU.add,
+            sums = small.tile([P, 2], F32)
+            nc.vector.tensor_reduce(
+                out=sums[:, 0:1], in_=position_sums[n][:], axis=X_AXIS, op=ALU.add
             )
-            moments = small.tile([P, 2], F32)
-            nc.vector.bn_aggr(out=moments[:], in_=stats[n][:].rearrange("p h q s -> p (h q s)"))
-            nc.vector.scalar_tensor_tensor(
-                out=moments[:, 1:2],
-                in0=moments[:, 0:1],
-                scalar=moments[:, 0:1],
-                in1=moments[:, 1:2],
-                op0=ALU.mult,
-                op1=ALU.add,
-            )
+            nc.vector.tensor_reduce(out=sums[:, 1:2], in_=square_sums[n][:], axis=X_AXIS, op=ALU.add)
             total_ps = psum_small.tile([P, 2], F32, tag="small")
             nc.tensor.matmul(
-                out=total_ps[:], lhsT=mean_over_partitions[:], rhs=moments[:], start=True, stop=True
+                out=total_ps[:], lhsT=mean_of_sample[:], rhs=sums[:], start=True, stop=True
             )
             return total_ps
 
@@ -210,7 +227,7 @@ def tile_prgselfatt_pa_t_kernel(tc, x, attn_out, w_out, b_out, out):
             shift = small.tile([P, HALVES], F32)
             nc.vector.tensor_scalar(
                 out=shift[:],
-                in0=b_col[:],
+                in0=b_centred[:],
                 scalar1=total[:, 0:1],
                 scalar2=rstd[:, 0:1],
                 op0=ALU.subtract,

@@ -23,7 +23,6 @@ PACK = 4
 COLS = 512
 CHUNKS = POSITIONS // COLS
 HALVES = C_OUT // P
-SCALAR_COLS = 80
 
 QUANTISE_LAG = 1
 SUM_LAG = 2
@@ -133,15 +132,10 @@ def tile_prgselfatt_pa_t_kernel(tc, x, attn_out, w_out, b_out, out):
 
         def regroup(n, q):
             grouped[(n, q)] = stage.tile([P, COLS, PACK], BF16, name="grouped", align_bytes=64)
-            rows = a_raw[n][:, :, q * COLS : (q + 1) * COLS]
-            for copy, first, last in (
-                (nc.scalar.copy, 0, SCALAR_COLS),
-                (nc.vector.tensor_copy, SCALAR_COLS, COLS),
-            ):
-                copy(
-                    out=grouped[(n, q)][:, first:last, :].rearrange("p (c i) j -> p c j i", i=4),
-                    in_=rows[:, :, first:last].rearrange("p j (c i) -> p c j i", i=4),
-                )
+            nc.vector.tensor_copy(
+                out=grouped[(n, q)][:].rearrange("p (c i) j -> p c j i", i=4),
+                in_=a_raw[n][:, :, q * COLS : (q + 1) * COLS].rearrange("p j (c i) -> p c j i", i=4),
+            )
 
         def quantise(n, q):
             cols = slice(q * COLS, (q + 1) * COLS)

@@ -23,10 +23,14 @@ PACK = 4
 COLS = 512
 CHUNKS = POSITIONS // COLS
 HALVES = C_OUT // P
+UNIT_BANKS = 2
+UNIT_COLS = UNIT_BANKS * COLS
+SCALAR_COLS = 80
 
 QUANTISE_LAG = 1
 SUM_LAG = 2
-NORMALISE_LAG = 9
+CHAIN_STEPS = 3
+NORMALISE_LAG = CHUNKS - 1 + SUM_LAG + CHAIN_STEPS + 1
 
 FLOPS = 2 * SAMPLES * C_OUT * C_IN * POSITIONS
 
@@ -43,32 +47,34 @@ def tile_prgselfatt_pa_t_kernel(tc, x, attn_out, w_out, b_out, out):
         psum_mean = ctx.enter_context(tc.psum_pool(name="psum_mean", bufs=2))
         psum_square = ctx.enter_context(tc.psum_pool(name="psum_square", bufs=2))
         psum_norm = ctx.enter_context(tc.psum_pool(name="psum_norm", bufs=3))
-        a_raw = []
+        ctx.enter_context(tc.manual_schedule())
+
+        a_raw = {}
         x_rows = []
         a_codes = []
         a_scales = []
         for n in range(SAMPLES):
-            a_raw.append(inputs.tile([P, PACK, POSITIONS], BF16, name="a_raw%d" % n))
+            for q in range(CHUNKS):
+                a_raw[(n, q)] = inputs.tile([P, PACK, COLS], BF16, name="a_raw%d_%d" % (n, q))
             x_rows.append(inputs.tile([P, HALVES, POSITIONS], BF16, name="x_rows%d" % n))
             a_codes.append(inputs.tile([P, POSITIONS], U32, name="a_codes%d" % n, align_bytes=64))
             a_scales.append(inputs.tile([P, POSITIONS], U8, name="a_scales%d" % n, align_bytes=64))
         w_rows = const.tile([P, HALVES, C_IN], BF16)
-        b_rows = const.tile([P, P], BF16)
-        nc.vector.memset(b_rows[:], 0.0)
+        b_rows = const.tile([P, HALVES], BF16)
 
         def load_a(n, q):
             cols = slice(q * COLS, (q + 1) * COLS)
             rows = attn_out[n].rearrange("(p j) t y w -> p j (t y w)", j=PACK)
-            nc.sync.dma_start(out=a_raw[n][:, :, cols], in_=rows[:, :, cols])
+            nc.sync.dma_start(out=a_raw[(n, q)][:], in_=rows[:, :, cols])
 
         def load_x(n):
             nc.sync.dma_start(
-                out=x_rows[n][:], in_=x[n].rearrange("(h c) t y w -> c h (t y w)", h=HALVES)
+                out=x_rows[n][:], in_=x[n].rearrange("(c h) t y w -> c h (t y w)", h=HALVES)
             )
 
         load_a(0, 0)
-        nc.sync.dma_start(out=w_rows[:], in_=w_out.rearrange("(h c) k -> c h k", h=HALVES))
-        nc.sync.dma_start(out=b_rows[0:HALVES, :], in_=b_out.rearrange("(h c) -> h c", h=HALVES))
+        nc.sync.dma_start(out=w_rows[:], in_=w_out.rearrange("(c h) k -> c h k", h=HALVES))
+        nc.sync.dma_start(out=b_rows[:], in_=b_out.rearrange("(c h) -> c h", h=HALVES))
         for chunk in range(1, SAMPLES * CHUNKS + NORMALISE_LAG):
             if chunk >= NORMALISE_LAG and (chunk - NORMALISE_LAG) % CHUNKS == 0:
                 load_x((chunk - NORMALISE_LAG) // CHUNKS)
@@ -83,59 +89,69 @@ def tile_prgselfatt_pa_t_kernel(tc, x, attn_out, w_out, b_out, out):
         nc.vector.memset(one[:], 1.0)
         nc.scalar.activation(out=one[:], in_=one[:], func=ACT.Sqrt)
 
-        w_words = (
-            w_rows[:]
-            .rearrange("c h k -> c (h k)")
-            .bitcast(F32)
-            .rearrange("c (h p u) -> c h u p", h=HALVES, u=2)
-        )
-        w_t = psum_small.tile([P, 2, C_OUT], F32, tag="small")
-        for h in range(HALVES):
-            for u in range(2):
-                nc.tensor.transpose(w_t[:, u, h * P : (h + 1) * P], w_words[:, h, u, :], ident[:])
+        b_col = const.tile([P, HALVES], F32)
+        b_mean = const.tile([P, 1], F32)
         w_grouped = const.tile([P, C_OUT * PACK], BF16, align_bytes=64)
-        nc.vector.tensor_copy(
-            out=w_grouped[:].bitcast(F32).rearrange("p (c u) -> p c u", u=2),
-            in_=w_t[:].rearrange("p u c -> p c u"),
-        )
         w_codes = const.tile([P, C_OUT], U32, align_bytes=64)
         w_scales = const.tile([P, C_OUT], U8, align_bytes=64)
-        nc.vector.quantize_mx(out=w_codes[:].bitcast(FP8X4), scales=w_scales[:], in_=w_grouped[:])
 
-        b_rows32 = const.tile([P, P], F32)
-        nc.vector.tensor_copy(out=b_rows32[:], in_=b_rows[:])
-        b_t = psum_small.tile([P, P], F32, tag="small")
-        nc.tensor.transpose(b_t[:], b_rows32[:], ident[:])
-        b_col = const.tile([P, HALVES], F32)
-        nc.vector.tensor_copy(out=b_col[:], in_=b_t[:, 0:HALVES])
-        b_mean_ps = psum_small.tile([P, HALVES], F32, tag="small")
-        nc.tensor.matmul(
-            out=b_mean_ps[:], lhsT=mean_of_sample[:], rhs=b_col[:], start=True, stop=True
-        )
-        b_mean = const.tile([P, 1], F32)
-        nc.vector.tensor_reduce(out=b_mean[:], in_=b_mean_ps[:], axis=X_AXIS, op=ALU.add)
-        b_centred = const.tile([P, HALVES], F32)
-        nc.vector.scalar_tensor_tensor(
-            out=b_centred[:],
-            in0=b_mean[:].to_broadcast([P, HALVES]),
-            scalar=-float(POSITIONS),
-            in1=b_col[:],
-            op0=ALU.mult,
-            op1=ALU.add,
-        )
+        def transpose_weights():
+            w_words = (
+                w_rows[:]
+                .rearrange("c h k -> c (h k)")
+                .bitcast(F32)
+                .rearrange("c (h p u) -> c h u p", h=HALVES, u=2)
+            )
+            w_t = psum_norm.tile([P, 2, C_OUT], F32, tag="product")
+            for h in range(HALVES):
+                for u in range(2):
+                    nc.tensor.transpose(
+                        w_t[:, u, h * P : (h + 1) * P], w_words[:, h, u, :], ident[:]
+                    )
+            nc.scalar.copy(
+                out=w_grouped[:].bitcast(F32).rearrange("p (c u) -> p c u", u=2),
+                in_=w_t[:].rearrange("p u c -> p c u"),
+            )
+
+        def widen_and_average_bias():
+            nc.scalar.copy(out=b_col[:], in_=b_rows[:])
+            b_mean_ps = psum_small.tile([P, HALVES], F32, tag="small")
+            nc.tensor.matmul(
+                out=b_mean_ps[:], lhsT=mean_of_sample[:], rhs=b_col[:], start=True, stop=True
+            )
+            b_mean_parts = const.tile([P, HALVES], F32)
+            nc.scalar.activation(
+                out=b_mean_parts[:],
+                in_=b_mean_ps[:],
+                func=ACT.Copy,
+                scale=float(POSITIONS),
+                accum_out=b_mean[:],
+            )
+
+        def quantise_weights():
+            nc.vector.quantize_mx(
+                out=w_codes[:].bitcast(FP8X4), scales=w_scales[:], in_=w_grouped[:]
+            )
 
         grouped = {}
         square_sums = {}
         position_sums = {}
-        totals = {}
+        sample_sums = {}
+        totals_ps = {}
+        moments = {}
+        deviation = {}
         scale_shift = {}
 
         def regroup(n, q):
             grouped[(n, q)] = stage.tile([P, COLS, PACK], BF16, name="grouped", align_bytes=64)
-            nc.vector.tensor_copy(
-                out=grouped[(n, q)][:].rearrange("p (c i) j -> p c j i", i=4),
-                in_=a_raw[n][:, :, q * COLS : (q + 1) * COLS].rearrange("p j (c i) -> p c j i", i=4),
-            )
+            for copy, first, last in (
+                (nc.scalar.copy, 0, SCALAR_COLS),
+                (nc.vector.tensor_copy, SCALAR_COLS, COLS),
+            ):
+                copy(
+                    out=grouped[(n, q)][:, first:last, :].rearrange("p (c i) j -> p c j i", i=4),
+                    in_=a_raw[(n, q)][:, :, first:last].rearrange("p j (c i) -> p c j i", i=4),
+                )
 
         def quantise(n, q):
             cols = slice(q * COLS, (q + 1) * COLS)
@@ -172,7 +188,7 @@ def tile_prgselfatt_pa_t_kernel(tc, x, attn_out, w_out, b_out, out):
                     out=squares[:],
                     in_=product[:],
                     func=ACT.Square,
-                    bias=b_centred[:, h : h + 1],
+                    bias=b_col[:, h : h + 1],
                     accum_out=square_sums[n][:, bank : bank + 1],
                 )
             for first in range(q * COLS, (q + 1) * COLS, P):
@@ -187,55 +203,68 @@ def tile_prgselfatt_pa_t_kernel(tc, x, attn_out, w_out, b_out, out):
                 )
 
         def sum_sample(n):
-            sums = small.tile([P, 2], F32)
+            sample_sums[n] = small.tile([P, 2], F32, name="sample_sums")
             nc.vector.tensor_reduce(
-                out=sums[:, 0:1], in_=position_sums[n][:], axis=X_AXIS, op=ALU.add
+                out=sample_sums[n][:, 0:1], in_=position_sums[n][:], axis=X_AXIS, op=ALU.add
             )
-            nc.vector.tensor_reduce(out=sums[:, 1:2], in_=square_sums[n][:], axis=X_AXIS, op=ALU.add)
-            total_ps = psum_small.tile([P, 2], F32, tag="small")
-            nc.tensor.matmul(
-                out=total_ps[:], lhsT=mean_of_sample[:], rhs=sums[:], start=True, stop=True
+            nc.vector.tensor_reduce(
+                out=sample_sums[n][:, 1:2], in_=square_sums[n][:], axis=X_AXIS, op=ALU.add
             )
-            return total_ps
 
-        def variance(n, total_ps):
-            total = small.tile([P, 2], F32)
-            nc.vector.tensor_copy(out=total[:], in_=total_ps[:])
+        def average(n):
+            totals_ps[n] = psum_small.tile([P, 2], F32, name="totals_ps", tag="small")
+            nc.tensor.matmul(
+                out=totals_ps[n][:],
+                lhsT=mean_of_sample[:],
+                rhs=sample_sums[n][:],
+                start=True,
+                stop=True,
+            )
+
+        def mean_and_variance(n):
+            mean = small.tile([P, 1], F32)
+            nc.vector.tensor_scalar_add(
+                out=mean[:], in0=totals_ps[n][:, 0:1], scalar1=b_mean[:, 0:1]
+            )
             neg_var = small.tile([P, 1], F32)
             nc.vector.scalar_tensor_tensor(
                 out=neg_var[:],
-                in0=total[:, 0:1],
-                scalar=total[:, 0:1],
-                in1=total[:, 1:2],
+                in0=mean[:],
+                scalar=mean[:, 0:1],
+                in1=totals_ps[n][:, 1:2],
                 op0=ALU.mult,
                 op1=ALU.subtract,
             )
-            totals[n] = (total, neg_var)
+            moments[n] = (mean, neg_var)
+
+        def standard_deviation(n):
+            deviation[n] = small.tile([P, 1], F32, name="deviation")
+            nc.scalar.activation(
+                out=deviation[n][:], in_=moments[n][1][:], func=ACT.Sqrt, scale=-1.0, bias=EPS
+            )
 
         def scale_and_shift(n):
-            total, neg_var = totals[n]
-            std = small.tile([P, 1], F32)
-            nc.scalar.activation(out=std[:], in_=neg_var[:], func=ACT.Sqrt, scale=-1.0, bias=EPS)
             rstd = small.tile([P, 1], F32)
-            nc.vector.reciprocal(out=rstd[:], in_=std[:])
+            nc.vector.reciprocal(out=rstd[:], in_=deviation[n][:])
             shift = small.tile([P, HALVES], F32)
             nc.vector.tensor_scalar(
                 out=shift[:],
-                in0=b_centred[:],
-                scalar1=total[:, 0:1],
+                in0=b_col[:],
+                scalar1=moments[n][0][:, 0:1],
                 scalar2=rstd[:, 0:1],
                 op0=ALU.subtract,
                 op1=ALU.mult,
             )
             scale_shift[n] = (rstd, shift)
 
-        def normalise(n, q):
+        def normalise(n, unit):
+            block, h = divmod(unit, HALVES)
             rstd, shift = scale_shift[n]
-            result = results.tile([P, HALVES, COLS], F32)
-            for h in range(HALVES):
-                product = multiply(psum_norm, n, q, h)
+            result = results.tile([P, UNIT_COLS], F32)
+            for i in range(UNIT_BANKS):
+                product = multiply(psum_norm, n, block * UNIT_BANKS + i, h)
                 nc.scalar.activation(
-                    out=result[:, h, :],
+                    out=result[:, i * COLS : (i + 1) * COLS],
                     in_=product[:],
                     func=ACT.Identity,
                     scale=rstd[:, 0:1],
@@ -243,37 +272,49 @@ def tile_prgselfatt_pa_t_kernel(tc, x, attn_out, w_out, b_out, out):
                 )
             return result
 
-        def add_x_and_store(n, q, result):
-            cols = slice(q * COLS, (q + 1) * COLS)
+        def add_x_and_store(n, unit, result):
+            block, h = divmod(unit, HALVES)
+            cols = slice(block * UNIT_COLS, (block + 1) * UNIT_COLS)
             nc.vector.tensor_tensor(
-                out=result[:], in0=result[:], in1=x_rows[n][:, :, cols], op=ALU.add
+                out=result[:], in0=result[:], in1=x_rows[n][:, h, cols], op=ALU.add
             )
             nc.sync.dma_start(
-                out=out[n].rearrange("(h c) t y w -> c h (t y w)", h=HALVES)[:, :, cols],
+                out=out[n].rearrange("(c h) t y w -> c h (t y w)", h=HALVES)[:, h, cols],
                 in_=result[:],
             )
 
         total_chunks = SAMPLES * CHUNKS
+
+        def summed(step, steps_ago):
+            n, q = divmod(step - SUM_LAG - steps_ago, CHUNKS)
+            return n if 0 <= n < SAMPLES and q == CHUNKS - 1 else None
+
         for step in range(total_chunks + NORMALISE_LAG):
-            to_regroup = step
             to_quantise = step - QUANTISE_LAG
             to_sum = step - SUM_LAG
             to_normalise = step - NORMALISE_LAG
 
-            if 0 <= to_quantise < total_chunks:
-                quantise(*divmod(to_quantise, CHUNKS))
-            if 0 <= to_sum - 2 < total_chunks and (to_sum - 2) % CHUNKS == CHUNKS - 1:
-                scale_and_shift((to_sum - 2) // CHUNKS)
+            if summed(step, 2) is not None:
+                average(summed(step, 2))
             if to_normalise >= 0:
                 result = normalise(*divmod(to_normalise, CHUNKS))
-            if to_regroup < total_chunks:
-                regroup(*divmod(to_regroup, CHUNKS))
-            sample_done = 0 <= to_sum < total_chunks and to_sum % CHUNKS == CHUNKS - 1
+            if step < total_chunks:
+                regroup(*divmod(step, CHUNKS))
+            if 0 <= to_quantise < total_chunks:
+                quantise(*divmod(to_quantise, CHUNKS))
+            if step == SUM_LAG - 2:
+                transpose_weights()
+                widen_and_average_bias()
+            if step == SUM_LAG - 1:
+                quantise_weights()
             if 0 <= to_sum < total_chunks:
                 sum_chunk(*divmod(to_sum, CHUNKS))
-            if sample_done:
-                total_ps = sum_sample(to_sum // CHUNKS)
+            if summed(step, 1) is not None:
+                sum_sample(summed(step, 1))
+            if summed(step, 2) is not None:
+                mean_and_variance(summed(step, 2))
+                standard_deviation(summed(step, 2))
+            if summed(step, 3) is not None:
+                scale_and_shift(summed(step, 3))
             if to_normalise >= 0:
                 add_x_and_store(*divmod(to_normalise, CHUNKS), result)
-            if sample_done:
-                variance(to_sum // CHUNKS, total_ps)

@@ -31,6 +31,7 @@ QUANTISE_LAG = 1
 SUM_LAG = 2
 CHAIN_STEPS = 3
 NORMALISE_LAG = CHUNKS - 1 + SUM_LAG + CHAIN_STEPS + 1
+LOAD_LEAD = 6
 
 FLOPS = 2 * SAMPLES * C_OUT * C_IN * POSITIONS
 
@@ -42,7 +43,7 @@ def tile_prgselfatt_pa_t_kernel(tc, x, attn_out, w_out, b_out, out):
         inputs = ctx.enter_context(tc.tile_pool(name="inputs", bufs=1))
         stage = ctx.enter_context(tc.tile_pool(name="stage", bufs=3))
         small = ctx.enter_context(tc.tile_pool(name="small", bufs=2))
-        results = ctx.enter_context(tc.tile_pool(name="results", bufs=6))
+        results = ctx.enter_context(tc.tile_pool(name="results", bufs=10))
         psum_small = ctx.enter_context(tc.psum_pool(name="psum_small", bufs=1))
         psum_mean = ctx.enter_context(tc.psum_pool(name="psum_mean", bufs=2))
         psum_square = ctx.enter_context(tc.psum_pool(name="psum_square", bufs=2))
@@ -72,14 +73,9 @@ def tile_prgselfatt_pa_t_kernel(tc, x, attn_out, w_out, b_out, out):
                 out=x_rows[n][:], in_=x[n].rearrange("(c h) t y w -> c h (t y w)", h=HALVES)
             )
 
-        load_a(0, 0)
-        nc.sync.dma_start(out=w_rows[:], in_=w_out.rearrange("(c h) k -> c h k", h=HALVES))
-        nc.sync.dma_start(out=b_rows[:], in_=b_out.rearrange("(c h) -> c h", h=HALVES))
-        for chunk in range(1, SAMPLES * CHUNKS + NORMALISE_LAG):
-            if chunk >= NORMALISE_LAG and (chunk - NORMALISE_LAG) % CHUNKS == 0:
-                load_x((chunk - NORMALISE_LAG) // CHUNKS)
-            if chunk < SAMPLES * CHUNKS:
-                load_a(*divmod(chunk, CHUNKS))
+        def load_weights_and_bias():
+            nc.sync.dma_start(out=w_rows[:], in_=w_out.rearrange("(c h) k -> c h k", h=HALVES))
+            nc.sync.dma_start(out=b_rows[:], in_=b_out.rearrange("(c h) -> c h", h=HALVES))
 
         ident = const.tile([P, P], F32)
         make_identity(nc, ident[:])
@@ -138,9 +134,10 @@ def tile_prgselfatt_pa_t_kernel(tc, x, attn_out, w_out, b_out, out):
         position_sums = {}
         sample_sums = {}
         totals_ps = {}
-        moments = {}
-        deviation = {}
-        scale_shift = {}
+        means = {}
+        deviations = {}
+        scales = {}
+        shifts = {}
 
         def regroup(n, q):
             grouped[(n, q)] = stage.tile([P, COLS, PACK], BF16, name="grouped", align_bytes=64)
@@ -179,7 +176,7 @@ def tile_prgselfatt_pa_t_kernel(tc, x, attn_out, w_out, b_out, out):
         def sum_chunk(n, q):
             if q == 0:
                 square_sums[n] = small.tile([P, CHUNKS * HALVES], F32, name="square_sums")
-                position_sums[n] = psum_mean.tile([P, C_OUT], F32, name="position_sums")
+                position_sums[n] = psum_mean.tile([P, P], F32, name="position_sums")
             for h in range(HALVES):
                 product = multiply(psum_square, n, q, h)
                 squares = stage.tile([P, COLS], BF16)
@@ -192,15 +189,16 @@ def tile_prgselfatt_pa_t_kernel(tc, x, attn_out, w_out, b_out, out):
                     accum_out=square_sums[n][:, bank : bank + 1],
                 )
             for first in range(q * COLS, (q + 1) * COLS, P):
-                nc.tensor.matmul_mx(
-                    out=position_sums[n][:],
-                    lhsT=a_codes[n][:, first : first + P].bitcast(FP8X4),
-                    lhsT_scale=a_scales[n][:, first : first + P],
-                    rhs=w_codes[:].bitcast(FP8X4),
-                    rhs_scale=w_scales[:],
-                    start=(first == 0),
-                    stop=(first + P == POSITIONS),
-                )
+                for h in range(HALVES):
+                    nc.tensor.matmul_mx(
+                        out=position_sums[n][:],
+                        lhsT=a_codes[n][:, first : first + P].bitcast(FP8X4),
+                        lhsT_scale=a_scales[n][:, first : first + P],
+                        rhs=w_codes[:, h * P : (h + 1) * P].bitcast(FP8X4),
+                        rhs_scale=w_scales[:, h * P : (h + 1) * P],
+                        start=(first == 0 and h == 0),
+                        stop=(first + P == POSITIONS and h == HALVES - 1),
+                    )
 
         def sum_sample(n):
             sample_sums[n] = small.tile([P, 2], F32, name="sample_sums")
@@ -221,45 +219,44 @@ def tile_prgselfatt_pa_t_kernel(tc, x, attn_out, w_out, b_out, out):
                 stop=True,
             )
 
-        def mean_and_variance(n):
-            mean = small.tile([P, 1], F32)
+        def mean_of(n):
+            means[n] = small.tile([P, 1], F32, name="mean")
             nc.vector.tensor_scalar_add(
-                out=mean[:], in0=totals_ps[n][:, 0:1], scalar1=b_mean[:, 0:1]
+                out=means[n][:], in0=totals_ps[n][:, 0:1], scalar1=b_mean[:, 0:1]
             )
+
+        def standard_deviation(n):
             neg_var = small.tile([P, 1], F32)
             nc.vector.scalar_tensor_tensor(
                 out=neg_var[:],
-                in0=mean[:],
-                scalar=mean[:, 0:1],
+                in0=means[n][:],
+                scalar=means[n][:, 0:1],
                 in1=totals_ps[n][:, 1:2],
                 op0=ALU.mult,
                 op1=ALU.subtract,
             )
-            moments[n] = (mean, neg_var)
-
-        def standard_deviation(n):
-            deviation[n] = small.tile([P, 1], F32, name="deviation")
+            deviations[n] = small.tile([P, 1], F32, name="deviation")
             nc.scalar.activation(
-                out=deviation[n][:], in_=moments[n][1][:], func=ACT.Sqrt, scale=-1.0, bias=EPS
+                out=deviations[n][:], in_=neg_var[:], func=ACT.Sqrt, scale=-1.0, bias=EPS
             )
 
-        def scale_and_shift(n):
-            rstd = small.tile([P, 1], F32)
-            nc.vector.reciprocal(out=rstd[:], in_=deviation[n][:])
-            shift = small.tile([P, HALVES], F32)
+        def scale_of(n):
+            scales[n] = small.tile([P, 1], F32, name="scale")
+            nc.vector.reciprocal(out=scales[n][:], in_=deviations[n][:])
+
+        def shift_of(n):
+            shifts[n] = small.tile([P, HALVES], F32, name="shift")
             nc.vector.tensor_scalar(
-                out=shift[:],
+                out=shifts[n][:],
                 in0=b_col[:],
-                scalar1=moments[n][0][:, 0:1],
-                scalar2=rstd[:, 0:1],
+                scalar1=means[n][:, 0:1],
+                scalar2=scales[n][:, 0:1],
                 op0=ALU.subtract,
                 op1=ALU.mult,
             )
-            scale_shift[n] = (rstd, shift)
 
         def normalise(n, unit):
             block, h = divmod(unit, HALVES)
-            rstd, shift = scale_shift[n]
             result = results.tile([P, UNIT_COLS], F32)
             for i in range(UNIT_BANKS):
                 product = multiply(psum_norm, n, block * UNIT_BANKS + i, h)
@@ -267,21 +264,24 @@ def tile_prgselfatt_pa_t_kernel(tc, x, attn_out, w_out, b_out, out):
                     out=result[:, i * COLS : (i + 1) * COLS],
                     in_=product[:],
                     func=ACT.Identity,
-                    scale=rstd[:, 0:1],
-                    bias=shift[:, h : h + 1],
+                    scale=scales[n][:, 0:1],
+                    bias=shifts[n][:, h : h + 1],
                 )
             return result
 
         def add_x_and_store(n, unit, result):
             block, h = divmod(unit, HALVES)
-            cols = slice(block * UNIT_COLS, (block + 1) * UNIT_COLS)
-            nc.vector.tensor_tensor(
-                out=result[:], in0=result[:], in1=x_rows[n][:, h, cols], op=ALU.add
-            )
-            nc.sync.dma_start(
-                out=out[n].rearrange("(c h) t y w -> c h (t y w)", h=HALVES)[:, h, cols],
-                in_=result[:],
-            )
+            pieces = UNIT_BANKS if (n, unit) == (SAMPLES - 1, CHUNKS - 1) else 1
+            width = UNIT_COLS // pieces
+            for piece in range(pieces):
+                part = result[:, piece * width : (piece + 1) * width]
+                first = block * UNIT_COLS + piece * width
+                cols = slice(first, first + width)
+                nc.vector.tensor_tensor(out=part, in0=part, in1=x_rows[n][:, h, cols], op=ALU.add)
+                nc.sync.dma_start(
+                    out=out[n].rearrange("(c h) t y w -> c h (t y w)", h=HALVES)[:, h, cols],
+                    in_=part,
+                )
 
         total_chunks = SAMPLES * CHUNKS
 
@@ -289,32 +289,42 @@ def tile_prgselfatt_pa_t_kernel(tc, x, attn_out, w_out, b_out, out):
             n, q = divmod(step - SUM_LAG - steps_ago, CHUNKS)
             return n if 0 <= n < SAMPLES and q == CHUNKS - 1 else None
 
-        for step in range(total_chunks + NORMALISE_LAG):
+        for step in range(-LOAD_LEAD, total_chunks + NORMALISE_LAG):
+            to_load = step + LOAD_LEAD
             to_quantise = step - QUANTISE_LAG
             to_sum = step - SUM_LAG
             to_normalise = step - NORMALISE_LAG
+
+            if to_load == SUM_LAG:
+                load_weights_and_bias()
+            if to_load - NORMALISE_LAG in range(0, total_chunks, CHUNKS):
+                load_x((to_load - NORMALISE_LAG) // CHUNKS)
+            if to_load < total_chunks:
+                load_a(*divmod(to_load, CHUNKS))
 
             if summed(step, 2) is not None:
                 average(summed(step, 2))
             if to_normalise >= 0:
                 result = normalise(*divmod(to_normalise, CHUNKS))
-            if step < total_chunks:
+            if 0 <= step < total_chunks:
                 regroup(*divmod(step, CHUNKS))
+            if summed(step, 2) is not None:
+                mean_of(summed(step, 2))
+            if summed(step, 3) is not None:
+                scale_of(summed(step, 3))
             if 0 <= to_quantise < total_chunks:
                 quantise(*divmod(to_quantise, CHUNKS))
-            if step == SUM_LAG - 2:
+            if step == SUM_LAG - 1:
                 transpose_weights()
                 widen_and_average_bias()
-            if step == SUM_LAG - 1:
                 quantise_weights()
             if 0 <= to_sum < total_chunks:
                 sum_chunk(*divmod(to_sum, CHUNKS))
             if summed(step, 1) is not None:
                 sum_sample(summed(step, 1))
             if summed(step, 2) is not None:
-                mean_and_variance(summed(step, 2))
                 standard_deviation(summed(step, 2))
             if summed(step, 3) is not None:
-                scale_and_shift(summed(step, 3))
+                shift_of(summed(step, 3))
             if to_normalise >= 0:
                 add_x_and_store(*divmod(to_normalise, CHUNKS), result)

@@ -22,6 +22,7 @@ P = 128
 PACK = 4
 COLS = 512
 CHUNKS = POSITIONS // COLS
+LOAD_CHUNKS = 2
 HALVES = C_OUT // P
 UNIT_BANKS = 2
 UNIT_COLS = UNIT_BANKS * COLS
@@ -55,8 +56,10 @@ def tile_prgselfatt_pa_t_kernel(tc, x, attn_out, w_out, b_out, out):
         a_codes = []
         a_scales = []
         for n in range(SAMPLES):
-            for q in range(CHUNKS):
-                a_raw[(n, q)] = inputs.tile([P, PACK, COLS], BF16, name="a_raw%d_%d" % (n, q))
+            for q in range(0, CHUNKS, LOAD_CHUNKS):
+                a_raw[(n, q)] = inputs.tile(
+                    [P, PACK, LOAD_CHUNKS * COLS], BF16, name="a_raw%d_%d" % (n, q)
+                )
             x_rows.append(inputs.tile([P, HALVES, POSITIONS], BF16, name="x_rows%d" % n))
             a_codes.append(inputs.tile([P, POSITIONS], U32, name="a_codes%d" % n, align_bytes=64))
             a_scales.append(inputs.tile([P, POSITIONS], U8, name="a_scales%d" % n, align_bytes=64))
@@ -64,7 +67,7 @@ def tile_prgselfatt_pa_t_kernel(tc, x, attn_out, w_out, b_out, out):
         b_rows = const.tile([P, HALVES], BF16)
 
         def load_a(n, q):
-            cols = slice(q * COLS, (q + 1) * COLS)
+            cols = slice(q * COLS, (q + LOAD_CHUNKS) * COLS)
             rows = attn_out[n].rearrange("(p j) t y w -> p j (t y w)", j=PACK)
             nc.sync.dma_start(out=a_raw[(n, q)][:], in_=rows[:, :, cols])
 
@@ -141,13 +144,14 @@ def tile_prgselfatt_pa_t_kernel(tc, x, attn_out, w_out, b_out, out):
 
         def regroup(n, q):
             grouped[(n, q)] = stage.tile([P, COLS, PACK], BF16, name="grouped", align_bytes=64)
+            rows = a_raw[(n, q - q % LOAD_CHUNKS)][:, :, (q % LOAD_CHUNKS) * COLS :]
             for copy, first, last in (
                 (nc.scalar.copy, 0, SCALAR_COLS),
                 (nc.vector.tensor_copy, SCALAR_COLS, COLS),
             ):
                 copy(
                     out=grouped[(n, q)][:, first:last, :].rearrange("p (c i) j -> p c j i", i=4),
-                    in_=a_raw[(n, q)][:, :, first:last].rearrange("p j (c i) -> p c j i", i=4),
+                    in_=rows[:, :, first:last].rearrange("p j (c i) -> p c j i", i=4),
                 )
 
         def quantise(n, q):
@@ -299,7 +303,7 @@ def tile_prgselfatt_pa_t_kernel(tc, x, attn_out, w_out, b_out, out):
                 load_weights_and_bias()
             if to_load - NORMALISE_LAG in range(0, total_chunks, CHUNKS):
                 load_x((to_load - NORMALISE_LAG) // CHUNKS)
-            if to_load < total_chunks:
+            if to_load < total_chunks and to_load % LOAD_CHUNKS == 0:
                 load_a(*divmod(to_load, CHUNKS))
 
             if summed(step, 2) is not None:

@@ -26,7 +26,8 @@ LOAD_CHUNKS = 2
 HALVES = C_OUT // P
 UNIT_BANKS = 2
 UNIT_COLS = UNIT_BANKS * COLS
-SCALAR_COLS = 80
+SCALAR_COLS_ALONE = 80
+SCALAR_COLS_BESIDE = 256
 
 QUANTISE_LAG = 1
 SUM_LAG = 2
@@ -142,12 +143,12 @@ def tile_prgselfatt_pa_t_kernel(tc, x, attn_out, w_out, b_out, out):
         scales = {}
         shifts = {}
 
-        def regroup(n, q):
+        def regroup(n, q, scalar_cols):
             grouped[(n, q)] = stage.tile([P, COLS, PACK], BF16, name="grouped", align_bytes=64)
             rows = a_raw[(n, q - q % LOAD_CHUNKS)][:, :, (q % LOAD_CHUNKS) * COLS :]
             for copy, first, last in (
-                (nc.scalar.copy, 0, SCALAR_COLS),
-                (nc.vector.tensor_copy, SCALAR_COLS, COLS),
+                (nc.scalar.copy, 0, scalar_cols),
+                (nc.vector.tensor_copy, scalar_cols, COLS),
             ):
                 copy(
                     out=grouped[(n, q)][:, first:last, :].rearrange("p (c i) j -> p c j i", i=4),
@@ -259,32 +260,45 @@ def tile_prgselfatt_pa_t_kernel(tc, x, attn_out, w_out, b_out, out):
                 op1=ALU.mult,
             )
 
-        def normalise(n, unit):
+        def shift_x(n, unit):
             block, h = divmod(unit, HALVES)
-            result = results.tile([P, UNIT_COLS], F32)
-            for i in range(UNIT_BANKS):
-                product = multiply(psum_norm, n, block * UNIT_BANKS + i, h)
-                nc.scalar.activation(
-                    out=result[:, i * COLS : (i + 1) * COLS],
-                    in_=product[:],
-                    func=ACT.Identity,
-                    scale=scales[n][:, 0:1],
-                    bias=shifts[n][:, h : h + 1],
-                )
+            cols = slice(block * UNIT_COLS, (block + 1) * UNIT_COLS)
+            result = results.tile([P, UNIT_COLS], F32, name="result")
+            nc.gpsimd.tensor_scalar(
+                out=result[:],
+                in0=x_rows[n][:, h, cols],
+                scalar1=1.0,
+                scalar2=shifts[n][:, h : h + 1],
+                op0=ALU.mult,
+                op1=ALU.add,
+            )
             return result
 
-        def add_x_and_store(n, unit, result):
+        def multiply_again(n, unit):
             block, h = divmod(unit, HALVES)
+            return [multiply(psum_norm, n, block * UNIT_BANKS + i, h) for i in range(UNIT_BANKS)]
+
+        def normalise_and_store(n, unit, products, result):
+            block, h = divmod(unit, HALVES)
+            for i in range(UNIT_BANKS):
+                part = result[:, i * COLS : (i + 1) * COLS]
+                nc.vector.scalar_tensor_tensor(
+                    out=part,
+                    in0=products[i][:],
+                    scalar=scales[n][:, 0:1],
+                    in1=part,
+                    op0=ALU.mult,
+                    op1=ALU.add,
+                )
             pieces = UNIT_BANKS if (n, unit) == (SAMPLES - 1, CHUNKS - 1) else 1
             width = UNIT_COLS // pieces
             for piece in range(pieces):
-                part = result[:, piece * width : (piece + 1) * width]
                 first = block * UNIT_COLS + piece * width
-                cols = slice(first, first + width)
-                nc.vector.tensor_tensor(out=part, in0=part, in1=x_rows[n][:, h, cols], op=ALU.add)
                 nc.sync.dma_start(
-                    out=out[n].rearrange("(c h) t y w -> c h (t y w)", h=HALVES)[:, h, cols],
-                    in_=part,
+                    out=out[n].rearrange("(c h) t y w -> c h (t y w)", h=HALVES)[
+                        :, h, first : first + width
+                    ],
+                    in_=result[:, piece * width : (piece + 1) * width],
                 )
 
         total_chunks = SAMPLES * CHUNKS
@@ -309,9 +323,12 @@ def tile_prgselfatt_pa_t_kernel(tc, x, attn_out, w_out, b_out, out):
             if summed(step, 2) is not None:
                 average(summed(step, 2))
             if to_normalise >= 0:
-                result = normalise(*divmod(to_normalise, CHUNKS))
+                result = shift_x(*divmod(to_normalise, CHUNKS))
             if 0 <= step < total_chunks:
-                regroup(*divmod(step, CHUNKS))
+                regroup(
+                    *divmod(step, CHUNKS),
+                    SCALAR_COLS_BESIDE if to_normalise >= 0 else SCALAR_COLS_ALONE,
+                )
             if summed(step, 2) is not None:
                 mean_of(summed(step, 2))
             if summed(step, 3) is not None:
@@ -331,4 +348,5 @@ def tile_prgselfatt_pa_t_kernel(tc, x, attn_out, w_out, b_out, out):
             if summed(step, 3) is not None:
                 shift_of(summed(step, 3))
             if to_normalise >= 0:
-                add_x_and_store(*divmod(to_normalise, CHUNKS), result)
+                products = multiply_again(*divmod(to_normalise, CHUNKS))
+                normalise_and_store(*divmod(to_normalise, CHUNKS), products, result)

@@ -28,6 +28,8 @@ UNIT_BANKS = 2
 UNIT_COLS = UNIT_BANKS * COLS
 SCALAR_COLS_ALONE = 80
 SCALAR_COLS_BESIDE = 256
+LATE_UNITS_FROM = 2 * CHUNKS
+LATE_SCALAR_COLS = 512
 
 QUANTISE_LAG = 1
 SUM_LAG = 2
@@ -53,14 +55,20 @@ def tile_prgselfatt_pa_t_kernel(tc, x, attn_out, w_out, b_out, out):
         ctx.enter_context(tc.manual_schedule())
 
         a_raw = {}
+        a_home = {}
         x_rows = []
         a_codes = []
         a_scales = []
         for n in range(SAMPLES):
             for q in range(0, CHUNKS, LOAD_CHUNKS):
-                a_raw[(n, q)] = inputs.tile(
-                    [P, PACK, LOAD_CHUNKS * COLS], BF16, name="a_raw%d_%d" % (n, q)
-                )
+                pieces = LOAD_CHUNKS if (n, q) == (0, 0) else 1
+                size = LOAD_CHUNKS // pieces
+                for first in range(q, q + LOAD_CHUNKS, size):
+                    a_raw[(n, first)] = inputs.tile(
+                        [P, PACK, size * COLS], BF16, name="a_raw%d_%d" % (n, first)
+                    )
+                    for place in range(size):
+                        a_home[(n, first + place)] = (first, place)
             x_rows.append(inputs.tile([P, HALVES, POSITIONS], BF16, name="x_rows%d" % n))
             a_codes.append(inputs.tile([P, POSITIONS], U32, name="a_codes%d" % n, align_bytes=64))
             a_scales.append(inputs.tile([P, POSITIONS], U8, name="a_scales%d" % n, align_bytes=64))
@@ -68,7 +76,7 @@ def tile_prgselfatt_pa_t_kernel(tc, x, attn_out, w_out, b_out, out):
         b_rows = const.tile([P, HALVES], BF16)
 
         def load_a(n, q):
-            cols = slice(q * COLS, (q + LOAD_CHUNKS) * COLS)
+            cols = slice(q * COLS, q * COLS + a_raw[(n, q)][:].shape[2])
             rows = attn_out[n].rearrange("(p j) t y w -> p j (t y w)", j=PACK)
             nc.sync.dma_start(out=a_raw[(n, q)][:], in_=rows[:, :, cols])
 
@@ -145,7 +153,8 @@ def tile_prgselfatt_pa_t_kernel(tc, x, attn_out, w_out, b_out, out):
 
         def regroup(n, q, scalar_cols):
             grouped[(n, q)] = stage.tile([P, COLS, PACK], BF16, name="grouped", align_bytes=64)
-            rows = a_raw[(n, q - q % LOAD_CHUNKS)][:, :, (q % LOAD_CHUNKS) * COLS :]
+            first_of_load, place = a_home[(n, q)]
+            rows = a_raw[(n, first_of_load)][:, :, place * COLS :]
             for copy, first, last in (
                 (nc.scalar.copy, 0, scalar_cols),
                 (nc.vector.tensor_copy, scalar_cols, COLS),
@@ -193,6 +202,8 @@ def tile_prgselfatt_pa_t_kernel(tc, x, attn_out, w_out, b_out, out):
                     bias=b_col[:, h : h + 1],
                     accum_out=square_sums[n][:, bank : bank + 1],
                 )
+
+        def sum_positions(n, q):
             for first in range(q * COLS, (q + 1) * COLS, P):
                 for h in range(HALVES):
                     nc.tensor.matmul_mx(
@@ -260,18 +271,26 @@ def tile_prgselfatt_pa_t_kernel(tc, x, attn_out, w_out, b_out, out):
                 op1=ALU.mult,
             )
 
-        def shift_x(n, unit):
+        def shift_x(n, unit, scalar_cols):
             block, h = divmod(unit, HALVES)
-            cols = slice(block * UNIT_COLS, (block + 1) * UNIT_COLS)
+            first = block * UNIT_COLS
+            split = UNIT_COLS - scalar_cols
             result = results.tile([P, UNIT_COLS], F32, name="result")
             nc.gpsimd.tensor_scalar(
-                out=result[:],
-                in0=x_rows[n][:, h, cols],
+                out=result[:, :split],
+                in0=x_rows[n][:, h, first : first + split],
                 scalar1=1.0,
                 scalar2=shifts[n][:, h : h + 1],
                 op0=ALU.mult,
                 op1=ALU.add,
             )
+            if scalar_cols:
+                nc.scalar.activation(
+                    out=result[:, split:],
+                    in_=x_rows[n][:, h, first + split : first + UNIT_COLS],
+                    func=ACT.Identity,
+                    bias=shifts[n][:, h : h + 1],
+                )
             return result
 
         def multiply_again(n, unit):
@@ -317,13 +336,13 @@ def tile_prgselfatt_pa_t_kernel(tc, x, attn_out, w_out, b_out, out):
                 load_weights_and_bias()
             if to_load - NORMALISE_LAG in range(0, total_chunks, CHUNKS):
                 load_x((to_load - NORMALISE_LAG) // CHUNKS)
-            if to_load < total_chunks and to_load % LOAD_CHUNKS == 0:
+            if divmod(to_load, CHUNKS) in a_raw:
                 load_a(*divmod(to_load, CHUNKS))
 
             if summed(step, 2) is not None:
                 average(summed(step, 2))
             if to_normalise >= 0:
-                result = shift_x(*divmod(to_normalise, CHUNKS))
+                result = shift_x(*divmod(to_normalise, CHUNKS), LATE_SCALAR_COLS if to_normalise >= LATE_UNITS_FROM else 0)
             if 0 <= step < total_chunks:
                 regroup(
                     *divmod(step, CHUNKS),
@@ -341,6 +360,10 @@ def tile_prgselfatt_pa_t_kernel(tc, x, attn_out, w_out, b_out, out):
                 quantise_weights()
             if 0 <= to_sum < total_chunks:
                 sum_chunk(*divmod(to_sum, CHUNKS))
+            if to_normalise >= 0:
+                products = multiply_again(*divmod(to_normalise, CHUNKS))
+            if 0 <= to_sum < total_chunks:
+                sum_positions(*divmod(to_sum, CHUNKS))
             if summed(step, 1) is not None:
                 sum_sample(summed(step, 1))
             if summed(step, 2) is not None:
@@ -348,5 +371,4 @@ def tile_prgselfatt_pa_t_kernel(tc, x, attn_out, w_out, b_out, out):
             if summed(step, 3) is not None:
                 shift_of(summed(step, 3))
             if to_normalise >= 0:
-                products = multiply_again(*divmod(to_normalise, CHUNKS))
                 normalise_and_store(*divmod(to_normalise, CHUNKS), products, result)

@@ -22,7 +22,8 @@ P = 128
 PACK = 4
 COLS = 512
 CHUNKS = POSITIONS // COLS
-LOAD_CHUNKS = 2
+LATER_LOADS = (1024, 1024)
+FIRST_LOADS = (256, 256, 512, 512, 512)
 HALVES = C_OUT // P
 UNIT_BANKS = 2
 UNIT_COLS = UNIT_BANKS * COLS
@@ -55,20 +56,19 @@ def tile_prgselfatt_pa_t_kernel(tc, x, attn_out, w_out, b_out, out):
         ctx.enter_context(tc.manual_schedule())
 
         a_raw = {}
-        a_home = {}
+        a_loads = []
         x_rows = []
         a_codes = []
         a_scales = []
         for n in range(SAMPLES):
-            for q in range(0, CHUNKS, LOAD_CHUNKS):
-                pieces = LOAD_CHUNKS if (n, q) == (0, 0) else 1
-                size = LOAD_CHUNKS // pieces
-                for first in range(q, q + LOAD_CHUNKS, size):
-                    a_raw[(n, first)] = inputs.tile(
-                        [P, PACK, size * COLS], BF16, name="a_raw%d_%d" % (n, first)
-                    )
-                    for place in range(size):
-                        a_home[(n, first + place)] = (first, place)
+            a_loads.append([])
+            first = 0
+            for width in FIRST_LOADS if n == 0 else LATER_LOADS:
+                a_loads[n].append((first, width))
+                a_raw[(n, first)] = inputs.tile(
+                    [P, PACK, width], BF16, name="a_raw%d_%d" % (n, first)
+                )
+                first += width
             x_rows.append(inputs.tile([P, HALVES, POSITIONS], BF16, name="x_rows%d" % n))
             a_codes.append(inputs.tile([P, POSITIONS], U32, name="a_codes%d" % n, align_bytes=64))
             a_scales.append(inputs.tile([P, POSITIONS], U8, name="a_scales%d" % n, align_bytes=64))
@@ -76,9 +76,14 @@ def tile_prgselfatt_pa_t_kernel(tc, x, attn_out, w_out, b_out, out):
         b_rows = const.tile([P, HALVES], BF16)
 
         def load_a(n, q):
-            cols = slice(q * COLS, q * COLS + a_raw[(n, q)][:].shape[2])
             rows = attn_out[n].rearrange("(p j) t y w -> p j (t y w)", j=PACK)
-            nc.sync.dma_start(out=a_raw[(n, q)][:], in_=rows[:, :, cols])
+            for first, width in a_loads[n]:
+                if first // COLS == q:
+                    nc.sync.dma_start(
+                        out=a_raw[(n, first)][:], in_=rows[:, :, first : first + width]
+                    )
+                    if (n, first) == (0, 0):
+                        load_weights_and_bias()
 
         def load_x(n):
             nc.sync.dma_start(
@@ -153,16 +158,23 @@ def tile_prgselfatt_pa_t_kernel(tc, x, attn_out, w_out, b_out, out):
 
         def regroup(n, q, scalar_cols):
             grouped[(n, q)] = stage.tile([P, COLS, PACK], BF16, name="grouped", align_bytes=64)
-            first_of_load, place = a_home[(n, q)]
-            rows = a_raw[(n, first_of_load)][:, :, place * COLS :]
-            for copy, first, last in (
+            for copy, share_first, share_last in (
                 (nc.scalar.copy, 0, scalar_cols),
                 (nc.vector.tensor_copy, scalar_cols, COLS),
             ):
-                copy(
-                    out=grouped[(n, q)][:, first:last, :].rearrange("p (c i) j -> p c j i", i=4),
-                    in_=rows[:, :, first:last].rearrange("p j (c i) -> p c j i", i=4),
-                )
+                for load_first, width in a_loads[n]:
+                    offset = q * COLS - load_first
+                    first = max(share_first, -offset)
+                    last = min(share_last, width - offset)
+                    if first < last:
+                        copy(
+                            out=grouped[(n, q)][:, first:last, :].rearrange(
+                                "p (c i) j -> p c j i", i=4
+                            ),
+                            in_=a_raw[(n, load_first)][
+                                :, :, offset + first : offset + last
+                            ].rearrange("p j (c i) -> p c j i", i=4),
+                        )
 
         def quantise(n, q):
             cols = slice(q * COLS, (q + 1) * COLS)
@@ -332,11 +344,9 @@ def tile_prgselfatt_pa_t_kernel(tc, x, attn_out, w_out, b_out, out):
             to_sum = step - SUM_LAG
             to_normalise = step - NORMALISE_LAG
 
-            if to_load == SUM_LAG:
-                load_weights_and_bias()
             if to_load - NORMALISE_LAG in range(0, total_chunks, CHUNKS):
                 load_x((to_load - NORMALISE_LAG) // CHUNKS)
-            if divmod(to_load, CHUNKS) in a_raw:
+            if 0 <= to_load < total_chunks:
                 load_a(*divmod(to_load, CHUNKS))
 
             if summed(step, 2) is not None:
@@ -354,7 +364,7 @@ def tile_prgselfatt_pa_t_kernel(tc, x, attn_out, w_out, b_out, out):
                 scale_of(summed(step, 3))
             if 0 <= to_quantise < total_chunks:
                 quantise(*divmod(to_quantise, CHUNKS))
-            if step == SUM_LAG - 1:
+            if step == 0:
                 transpose_weights()
                 widen_and_average_bias()
                 quantise_weights()

@@ -344,10 +344,14 @@ def tile_prgselfatt_pa_t_kernel(tc, x, attn_out, w_out, b_out, out):
             to_sum = step - SUM_LAG
             to_normalise = step - NORMALISE_LAG
 
-            if to_load - NORMALISE_LAG in range(0, total_chunks, CHUNKS):
+            if to_load - NORMALISE_LAG in range(0, total_chunks, CHUNKS) and to_load < total_chunks - 1:
                 load_x((to_load - NORMALISE_LAG) // CHUNKS)
             if 0 <= to_load < total_chunks:
                 load_a(*divmod(to_load, CHUNKS))
+            if to_load == total_chunks - 1:
+                for n in range(SAMPLES):
+                    if n * CHUNKS + NORMALISE_LAG >= total_chunks - 1:
+                        load_x(n)
 
             if summed(step, 2) is not None:
                 average(summed(step, 2))

@@ -100,10 +100,11 @@ def tile_prgselfatt_pa_t_kernel(tc, x, attn_out, w_out, b_out, out):
         nc.vector.memset(mean_of_sample[:], 1.0 / (C_OUT * POSITIONS))
         one = const.tile([P, 1], F32)
         nc.vector.memset(one[:], 1.0)
-        nc.scalar.activation(out=one[:], in_=one[:], func=ACT.Sqrt)
+        nc.scalar.activation(out=one[:], in_=one[:], func=ACT.Abs_reciprocal_sqrt)
 
         b_col = const.tile([P, HALVES], F32)
-        b_mean = const.tile([P, 1], F32)
+        b_sums = const.tile([P, 2], F32)
+        nc.vector.memset(b_sums[:], 0.0)
         w_grouped = const.tile([P, C_OUT * PACK], BF16, align_bytes=64)
         w_codes = const.tile([P, C_OUT], U32, align_bytes=64)
         w_scales = const.tile([P, C_OUT], U8, align_bytes=64)
@@ -128,17 +129,13 @@ def tile_prgselfatt_pa_t_kernel(tc, x, attn_out, w_out, b_out, out):
 
         def widen_and_average_bias():
             nc.scalar.copy(out=b_col[:], in_=b_rows[:])
-            b_mean_ps = psum_small.tile([P, HALVES], F32, tag="small")
-            nc.tensor.matmul(
-                out=b_mean_ps[:], lhsT=mean_of_sample[:], rhs=b_col[:], start=True, stop=True
-            )
-            b_mean_parts = const.tile([P, HALVES], F32)
+            b_parts = const.tile([P, HALVES], F32)
             nc.scalar.activation(
-                out=b_mean_parts[:],
-                in_=b_mean_ps[:],
+                out=b_parts[:],
+                in_=b_rows[:],
                 func=ACT.Copy,
                 scale=float(POSITIONS),
-                accum_out=b_mean[:],
+                accum_out=b_sums[:, 0:1],
             )
 
         def quantise_weights():
@@ -151,8 +148,6 @@ def tile_prgselfatt_pa_t_kernel(tc, x, attn_out, w_out, b_out, out):
         position_sums = {}
         sample_sums = {}
         totals_ps = {}
-        means = {}
-        deviations = {}
         scales = {}
         shifts = {}
 
@@ -240,44 +235,37 @@ def tile_prgselfatt_pa_t_kernel(tc, x, attn_out, w_out, b_out, out):
         def average(n):
             totals_ps[n] = psum_small.tile([P, 2], F32, name="totals_ps", tag="small")
             nc.tensor.matmul(
+                out=totals_ps[n][:], lhsT=mean_of_sample[:], rhs=b_sums[:], start=True, stop=False
+            )
+            nc.tensor.matmul(
                 out=totals_ps[n][:],
                 lhsT=mean_of_sample[:],
                 rhs=sample_sums[n][:],
-                start=True,
+                start=False,
                 stop=True,
             )
 
-        def mean_of(n):
-            means[n] = small.tile([P, 1], F32, name="mean")
-            nc.vector.tensor_scalar_add(
-                out=means[n][:], in0=totals_ps[n][:, 0:1], scalar1=b_mean[:, 0:1]
-            )
-
-        def standard_deviation(n):
-            neg_var = small.tile([P, 1], F32)
-            nc.vector.scalar_tensor_tensor(
+        def scale_of(n):
+            neg_var = small.tile([P, 1], F32, name="neg_var")
+            nc.vector.tensor_scalar(
                 out=neg_var[:],
-                in0=means[n][:],
-                scalar=means[n][:, 0:1],
-                in1=totals_ps[n][:, 1:2],
+                in0=totals_ps[n][:, 0:1],
+                scalar1=totals_ps[n][:, 0:1],
+                scalar2=totals_ps[n][:, 1:2],
                 op0=ALU.mult,
                 op1=ALU.subtract,
             )
-            deviations[n] = small.tile([P, 1], F32, name="deviation")
-            nc.scalar.activation(
-                out=deviations[n][:], in_=neg_var[:], func=ACT.Sqrt, scale=-1.0, bias=EPS
-            )
-
-        def scale_of(n):
             scales[n] = small.tile([P, 1], F32, name="scale")
-            nc.vector.reciprocal(out=scales[n][:], in_=deviations[n][:])
+            nc.scalar.activation(
+                out=scales[n][:], in_=neg_var[:], func=ACT.Abs_reciprocal_sqrt, bias=-EPS
+            )
 
         def shift_of(n):
             shifts[n] = small.tile([P, HALVES], F32, name="shift")
             nc.vector.tensor_scalar(
                 out=shifts[n][:],
                 in0=b_col[:],
-                scalar1=means[n][:, 0:1],
+                scalar1=totals_ps[n][:, 0:1],
                 scalar2=scales[n][:, 0:1],
                 op0=ALU.subtract,
                 op1=ALU.mult,
@@ -363,9 +351,9 @@ def tile_prgselfatt_pa_t_kernel(tc, x, attn_out, w_out, b_out, out):
                     SCALAR_COLS_BESIDE if to_normalise >= 0 else SCALAR_COLS_ALONE,
                 )
             if summed(step, 2) is not None:
-                mean_of(summed(step, 2))
+                scale_of(summed(step, 2))
             if summed(step, 3) is not None:
-                scale_of(summed(step, 3))
+                shift_of(summed(step, 3))
             if 0 <= to_quantise < total_chunks:
                 quantise(*divmod(to_quantise, CHUNKS))
             if step == 0:
@@ -380,9 +368,5 @@ def tile_prgselfatt_pa_t_kernel(tc, x, attn_out, w_out, b_out, out):
                 sum_positions(*divmod(to_sum, CHUNKS))
             if summed(step, 1) is not None:
                 sum_sample(summed(step, 1))
-            if summed(step, 2) is not None:
-                standard_deviation(summed(step, 2))
-            if summed(step, 3) is not None:
-                shift_of(summed(step, 3))
             if to_normalise >= 0:
                 normalise_and_store(*divmod(to_normalise, CHUNKS), products, result)

@@ -46,13 +46,12 @@ def tile_prgselfatt_pa_t_kernel(tc, x, attn_out, w_out, b_out, out):
     with ExitStack() as ctx:
         const = ctx.enter_context(tc.tile_pool(name="const", bufs=1))
         inputs = ctx.enter_context(tc.tile_pool(name="inputs", bufs=1))
-        stage = ctx.enter_context(tc.tile_pool(name="stage", bufs=3))
+        stage = ctx.enter_context(tc.tile_pool(name="stage", bufs=5))
         small = ctx.enter_context(tc.tile_pool(name="small", bufs=2))
         results = ctx.enter_context(tc.tile_pool(name="results", bufs=10))
         psum_small = ctx.enter_context(tc.psum_pool(name="psum_small", bufs=1))
         psum_mean = ctx.enter_context(tc.psum_pool(name="psum_mean", bufs=2))
-        psum_square = ctx.enter_context(tc.psum_pool(name="psum_square", bufs=2))
-        psum_norm = ctx.enter_context(tc.psum_pool(name="psum_norm", bufs=3))
+        psum_products = ctx.enter_context(tc.psum_pool(name="psum_products", bufs=5))
         ctx.enter_context(tc.manual_schedule())
 
         a_raw = {}
@@ -116,7 +115,7 @@ def tile_prgselfatt_pa_t_kernel(tc, x, attn_out, w_out, b_out, out):
                 .bitcast(F32)
                 .rearrange("c (h p u) -> c h u p", h=HALVES, u=2)
             )
-            w_t = psum_norm.tile([P, 2, C_OUT], F32, tag="product")
+            w_t = psum_products.tile([P, 2, C_OUT], F32, tag="product")
             for h in range(HALVES):
                 for u in range(2):
                     nc.tensor.transpose(
@@ -199,7 +198,7 @@ def tile_prgselfatt_pa_t_kernel(tc, x, attn_out, w_out, b_out, out):
                 square_sums[n] = small.tile([P, CHUNKS * HALVES], F32, name="square_sums")
                 position_sums[n] = psum_mean.tile([P, P], F32, name="position_sums")
             for h in range(HALVES):
-                product = multiply(psum_square, n, q, h)
+                product = multiply(psum_products, n, q, h)
                 squares = stage.tile([P, COLS], BF16)
                 bank = q * HALVES + h
                 nc.scalar.activation(
@@ -295,7 +294,7 @@ def tile_prgselfatt_pa_t_kernel(tc, x, attn_out, w_out, b_out, out):
 
         def multiply_again(n, unit):
             block, h = divmod(unit, HALVES)
-            return [multiply(psum_norm, n, block * UNIT_BANKS + i, h) for i in range(UNIT_BANKS)]
+            return [multiply(psum_products, n, block * UNIT_BANKS + i, h) for i in range(UNIT_BANKS)]
 
         def normalise_and_store(n, unit, products, result):
             block, h = divmod(unit, HALVES)

@@ -28,7 +28,7 @@ HALVES = C_OUT // P
 UNIT_BANKS = 2
 UNIT_COLS = UNIT_BANKS * COLS
 SCALAR_COLS_ALONE = 80
-SCALAR_COLS_BESIDE = 256
+SCALAR_COLS_BESIDE = 240
 LATE_UNITS_FROM = 2 * CHUNKS
 LATE_SCALAR_COLS = 512
 

from contextlib import ExitStack

import concourse.mybir as mybir
from concourse.masks import make_identity

F32 = mybir.dt.float32
BF16 = mybir.dt.bfloat16
U32 = mybir.dt.uint32
U8 = mybir.dt.uint8
FP8X4 = mybir.dt.float8_e4m3fn_x4
ACT = mybir.ActivationFunctionType
ALU = mybir.AluOpType
X_AXIS = mybir.AxisListType.X

SAMPLES = 4
C_IN = 512
C_OUT = 256
POSITIONS = 2048
EPS = 1e-5

P = 128
PACK = 4
COLS = 512
CHUNKS = POSITIONS // COLS
LATER_LOADS = (1024, 1024)
FIRST_LOADS = (256, 256, 512, 512, 512)
HALVES = C_OUT // P
UNIT_BANKS = 2
UNIT_COLS = UNIT_BANKS * COLS
SCALAR_COLS_ALONE = 80
SCALAR_COLS_BESIDE = 240
LATE_UNITS_FROM = 2 * CHUNKS
LATE_SCALAR_COLS = 512

QUANTISE_LAG = 1
SUM_LAG = 2
CHAIN_STEPS = 3
NORMALISE_LAG = CHUNKS - 1 + SUM_LAG + CHAIN_STEPS + 1
LOAD_LEAD = 6

FLOPS = 2 * SAMPLES * C_OUT * C_IN * POSITIONS


def tile_prgselfatt_pa_t_kernel(tc, x, attn_out, w_out, b_out, out):
    nc = tc.nc
    with ExitStack() as ctx:
        const = ctx.enter_context(tc.tile_pool(name="const", bufs=1))
        inputs = ctx.enter_context(tc.tile_pool(name="inputs", bufs=1))
        stage = ctx.enter_context(tc.tile_pool(name="stage", bufs=5))
        small = ctx.enter_context(tc.tile_pool(name="small", bufs=2))
        results = ctx.enter_context(tc.tile_pool(name="results", bufs=10))
        psum_small = ctx.enter_context(tc.psum_pool(name="psum_small", bufs=1))
        psum_mean = ctx.enter_context(tc.psum_pool(name="psum_mean", bufs=2))
        psum_products = ctx.enter_context(tc.psum_pool(name="psum_products", bufs=5))
        ctx.enter_context(tc.manual_schedule())

        a_raw = {}
        a_loads = []
        x_rows = []
        a_codes = []
        a_scales = []
        for n in range(SAMPLES):
            a_loads.append([])
            first = 0
            for width in FIRST_LOADS if n == 0 else LATER_LOADS:
                a_loads[n].append((first, width))
                a_raw[(n, first)] = inputs.tile(
                    [P, PACK, width], BF16, name="a_raw%d_%d" % (n, first)
                )
                first += width
            x_rows.append(inputs.tile([P, HALVES, POSITIONS], BF16, name="x_rows%d" % n))
            a_codes.append(inputs.tile([P, POSITIONS], U32, name="a_codes%d" % n, align_bytes=64))
            a_scales.append(inputs.tile([P, POSITIONS], U8, name="a_scales%d" % n, align_bytes=64))
        w_rows = const.tile([P, HALVES, C_IN], BF16)
        b_rows = const.tile([P, HALVES], BF16)

        def load_a(n, q):
            rows = attn_out[n].rearrange("(p j) t y w -> p j (t y w)", j=PACK)
            for first, width in a_loads[n]:
                if first // COLS == q:
                    nc.sync.dma_start(
                        out=a_raw[(n, first)][:], in_=rows[:, :, first : first + width]
                    )
                    if (n, first) == (0, 0):
                        load_weights_and_bias()

        def load_x(n):
            nc.sync.dma_start(
                out=x_rows[n][:], in_=x[n].rearrange("(c h) t y w -> c h (t y w)", h=HALVES)
            )

        def load_weights_and_bias():
            nc.sync.dma_start(out=w_rows[:], in_=w_out.rearrange("(c h) k -> c h k", h=HALVES))
            nc.sync.dma_start(out=b_rows[:], in_=b_out.rearrange("(c h) -> c h", h=HALVES))

        ident = const.tile([P, P], F32)
        make_identity(nc, ident[:])
        mean_of_sample = const.tile([P, P], F32)
        nc.vector.memset(mean_of_sample[:], 1.0 / (C_OUT * POSITIONS))
        one = const.tile([P, 1], F32)
        nc.vector.memset(one[:], 1.0)
        nc.scalar.activation(out=one[:], in_=one[:], func=ACT.Abs_reciprocal_sqrt)

        b_col = const.tile([P, HALVES], F32)
        b_sums = const.tile([P, 2], F32)
        nc.vector.memset(b_sums[:], 0.0)
        w_grouped = const.tile([P, C_OUT * PACK], BF16, align_bytes=64)
        w_codes = const.tile([P, C_OUT], U32, align_bytes=64)
        w_scales = const.tile([P, C_OUT], U8, align_bytes=64)

        def transpose_weights():
            w_words = (
                w_rows[:]
                .rearrange("c h k -> c (h k)")
                .bitcast(F32)
                .rearrange("c (h p u) -> c h u p", h=HALVES, u=2)
            )
            w_t = psum_products.tile([P, 2, C_OUT], F32, tag="product")
            for h in range(HALVES):
                for u in range(2):
                    nc.tensor.transpose(
                        w_t[:, u, h * P : (h + 1) * P], w_words[:, h, u, :], ident[:]
                    )
            nc.scalar.copy(
                out=w_grouped[:].bitcast(F32).rearrange("p (c u) -> p c u", u=2),
                in_=w_t[:].rearrange("p u c -> p c u"),
            )

        def widen_and_average_bias():
            nc.scalar.copy(out=b_col[:], in_=b_rows[:])
            b_parts = const.tile([P, HALVES], F32)
            nc.scalar.activation(
                out=b_parts[:],
                in_=b_rows[:],
                func=ACT.Copy,
                scale=float(POSITIONS),
                accum_out=b_sums[:, 0:1],
            )

        def quantise_weights():
            nc.vector.quantize_mx(
                out=w_codes[:].bitcast(FP8X4), scales=w_scales[:], in_=w_grouped[:]
            )

        grouped = {}
        square_sums = {}
        position_sums = {}
        sample_sums = {}
        totals_ps = {}
        scales = {}
        shifts = {}

        def regroup(n, q, scalar_cols):
            grouped[(n, q)] = stage.tile([P, COLS, PACK], BF16, name="grouped", align_bytes=64)
            for copy, share_first, share_last in (
                (nc.scalar.copy, 0, scalar_cols),
                (nc.vector.tensor_copy, scalar_cols, COLS),
            ):
                for load_first, width in a_loads[n]:
                    offset = q * COLS - load_first
                    first = max(share_first, -offset)
                    last = min(share_last, width - offset)
                    if first < last:
                        copy(
                            out=grouped[(n, q)][:, first:last, :].rearrange(
                                "p (c i) j -> p c j i", i=4
                            ),
                            in_=a_raw[(n, load_first)][
                                :, :, offset + first : offset + last
                            ].rearrange("p j (c i) -> p c j i", i=4),
                        )

        def quantise(n, q):
            cols = slice(q * COLS, (q + 1) * COLS)
            nc.vector.quantize_mx(
                out=a_codes[n][:, cols].bitcast(FP8X4),
                scales=a_scales[n][:, cols],
                in_=grouped[(n, q)][:].rearrange("p w j -> p (w j)"),
            )

        def multiply(pool, n, q, h):
            cols = slice(q * COLS, (q + 1) * COLS)
            channels = slice(h * P, (h + 1) * P)
            product = pool.tile([P, COLS], F32, name="product")
            nc.tensor.matmul_mx(
                out=product[:],
                lhsT=w_codes[:, channels].bitcast(FP8X4),
                lhsT_scale=w_scales[:, channels],
                rhs=a_codes[n][:, cols].bitcast(FP8X4),
                rhs_scale=a_scales[n][:, cols],
                start=True,
                stop=True,
            )
            return product

        def sum_chunk(n, q):
            if q == 0:
                square_sums[n] = small.tile([P, CHUNKS * HALVES], F32, name="square_sums")
                position_sums[n] = psum_mean.tile([P, P], F32, name="position_sums")
            for h in range(HALVES):
                product = multiply(psum_products, n, q, h)
                squares = stage.tile([P, COLS], BF16)
                bank = q * HALVES + h
                nc.scalar.activation(
                    out=squares[:],
                    in_=product[:],
                    func=ACT.Square,
                    bias=b_col[:, h : h + 1],
                    accum_out=square_sums[n][:, bank : bank + 1],
                )

        def sum_positions(n, q):
            for first in range(q * COLS, (q + 1) * COLS, P):
                for h in range(HALVES):
                    nc.tensor.matmul_mx(
                        out=position_sums[n][:],
                        lhsT=a_codes[n][:, first : first + P].bitcast(FP8X4),
                        lhsT_scale=a_scales[n][:, first : first + P],
                        rhs=w_codes[:, h * P : (h + 1) * P].bitcast(FP8X4),
                        rhs_scale=w_scales[:, h * P : (h + 1) * P],
                        start=(first == 0 and h == 0),
                        stop=(first + P == POSITIONS and h == HALVES - 1),
                    )

        def sum_sample(n):
            sample_sums[n] = small.tile([P, 2], F32, name="sample_sums")
            nc.vector.tensor_reduce(
                out=sample_sums[n][:, 0:1], in_=position_sums[n][:], axis=X_AXIS, op=ALU.add
            )
            nc.vector.tensor_reduce(
                out=sample_sums[n][:, 1:2], in_=square_sums[n][:], axis=X_AXIS, op=ALU.add
            )

        def average(n):
            totals_ps[n] = psum_small.tile([P, 2], F32, name="totals_ps", tag="small")
            nc.tensor.matmul(
                out=totals_ps[n][:], lhsT=mean_of_sample[:], rhs=b_sums[:], start=True, stop=False
            )
            nc.tensor.matmul(
                out=totals_ps[n][:],
                lhsT=mean_of_sample[:],
                rhs=sample_sums[n][:],
                start=False,
                stop=True,
            )

        def scale_of(n):
            neg_var = small.tile([P, 1], F32, name="neg_var")
            nc.vector.tensor_scalar(
                out=neg_var[:],
                in0=totals_ps[n][:, 0:1],
                scalar1=totals_ps[n][:, 0:1],
                scalar2=totals_ps[n][:, 1:2],
                op0=ALU.mult,
                op1=ALU.subtract,
            )
            scales[n] = small.tile([P, 1], F32, name="scale")
            nc.scalar.activation(
                out=scales[n][:], in_=neg_var[:], func=ACT.Abs_reciprocal_sqrt, bias=-EPS
            )

        def shift_of(n):
            shifts[n] = small.tile([P, HALVES], F32, name="shift")
            nc.vector.tensor_scalar(
                out=shifts[n][:],
                in0=b_col[:],
                scalar1=totals_ps[n][:, 0:1],
                scalar2=scales[n][:, 0:1],
                op0=ALU.subtract,
                op1=ALU.mult,
            )

        def shift_x(n, unit, scalar_cols):
            block, h = divmod(unit, HALVES)
            first = block * UNIT_COLS
            split = UNIT_COLS - scalar_cols
            result = results.tile([P, UNIT_COLS], F32, name="result")
            nc.gpsimd.tensor_scalar(
                out=result[:, :split],
                in0=x_rows[n][:, h, first : first + split],
                scalar1=1.0,
                scalar2=shifts[n][:, h : h + 1],
                op0=ALU.mult,
                op1=ALU.add,
            )
            if scalar_cols:
                nc.scalar.activation(
                    out=result[:, split:],
                    in_=x_rows[n][:, h, first + split : first + UNIT_COLS],
                    func=ACT.Identity,
                    bias=shifts[n][:, h : h + 1],
                )
            return result

        def multiply_again(n, unit):
            block, h = divmod(unit, HALVES)
            return [multiply(psum_products, n, block * UNIT_BANKS + i, h) for i in range(UNIT_BANKS)]

        def normalise_and_store(n, unit, products, result):
            block, h = divmod(unit, HALVES)
            for i in range(UNIT_BANKS):
                part = result[:, i * COLS : (i + 1) * COLS]
                nc.vector.scalar_tensor_tensor(
                    out=part,
                    in0=products[i][:],
                    scalar=scales[n][:, 0:1],
                    in1=part,
                    op0=ALU.mult,
                    op1=ALU.add,
                )
            pieces = UNIT_BANKS if (n, unit) == (SAMPLES - 1, CHUNKS - 1) else 1
            width = UNIT_COLS // pieces
            for piece in range(pieces):
                first = block * UNIT_COLS + piece * width
                nc.sync.dma_start(
                    out=out[n].rearrange("(c h) t y w -> c h (t y w)", h=HALVES)[
                        :, h, first : first + width
                    ],
                    in_=result[:, piece * width : (piece + 1) * width],
                )

        total_chunks = SAMPLES * CHUNKS

        def summed(step, steps_ago):
            n, q = divmod(step - SUM_LAG - steps_ago, CHUNKS)
            return n if 0 <= n < SAMPLES and q == CHUNKS - 1 else None

        for step in range(-LOAD_LEAD, total_chunks + NORMALISE_LAG):
            to_load = step + LOAD_LEAD
            to_quantise = step - QUANTISE_LAG
            to_sum = step - SUM_LAG
            to_normalise = step - NORMALISE_LAG

            if to_load - NORMALISE_LAG in range(0, total_chunks, CHUNKS) and to_load < total_chunks - 1:
                load_x((to_load - NORMALISE_LAG) // CHUNKS)
            if 0 <= to_load < total_chunks:
                load_a(*divmod(to_load, CHUNKS))
            if to_load == total_chunks - 1:
                for n in range(SAMPLES):
                    if n * CHUNKS + NORMALISE_LAG >= total_chunks - 1:
                        load_x(n)

            if summed(step, 2) is not None:
                average(summed(step, 2))
            if to_normalise >= 0:
                result = shift_x(*divmod(to_normalise, CHUNKS), LATE_SCALAR_COLS if to_normalise >= LATE_UNITS_FROM else 0)
            if 0 <= step < total_chunks:
                regroup(
                    *divmod(step, CHUNKS),
                    SCALAR_COLS_BESIDE if to_normalise >= 0 else SCALAR_COLS_ALONE,
                )
            if summed(step, 2) is not None:
                scale_of(summed(step, 2))
            if summed(step, 3) is not None:
                shift_of(summed(step, 3))
            if 0 <= to_quantise < total_chunks:
                quantise(*divmod(to_quantise, CHUNKS))
            if step == 0:
                transpose_weights()
                widen_and_average_bias()
                quantise_weights()
            if 0 <= to_sum < total_chunks:
                sum_chunk(*divmod(to_sum, CHUNKS))
            if to_normalise >= 0:
                products = multiply_again(*divmod(to_normalise, CHUNKS))
            if 0 <= to_sum < total_chunks:
                sum_positions(*divmod(to_sum, CHUNKS))
            if summed(step, 1) is not None:
                sum_sample(summed(step, 1))
            if to_normalise >= 0:
                normalise_and_store(*divmod(to_normalise, CHUNKS), products, result)
